import numpy as np
import ml_dtypes


def mxq(x, axis, fmt="e4m3"):
    dtype, down = {"e4m3": (ml_dtypes.float8_e4m3fn, 7), "e5m2": (ml_dtypes.float8_e5m2, 14)}[fmt]
    v = np.moveaxis(np.asarray(x, np.float32).astype(ml_dtypes.bfloat16).astype(np.float64), axis, -1)
    blocks = v.reshape(v.shape[:-1] + (-1, 32))
    amax = np.abs(blocks).max(-1, keepdims=True)
    byte = np.maximum(np.where(amax > 0, np.frexp(amax)[1] - 1 + 127, 0) - down, 1)
    scale = np.exp2(byte - 127.0)
    codes = (blocks / scale).astype(np.float32).astype(dtype).astype(np.float64)
    return np.moveaxis((codes * scale).reshape(v.shape), -1, axis)


WIDE = False


def mx_kscale(k):
    if not WIDE:
        return np.ones(k)
    levels = np.array([10, -10, 5, -5, 0])
    a = np.random.permutation(np.resize(levels, k // 512 * 4)).reshape(k // 512, 4)
    idx = np.arange(k)
    return np.exp2(a[idx // 512, idx % 128 // 32])


BF16 = ml_dtypes.bfloat16


def bf(x):
    return np.asarray(x, np.float32).astype(BF16)


def f64(x):
    return np.asarray(x).astype(np.float64)


B, CIN, H, W, CP, G = 3, 2048, 16, 16, 1024, 2
CG = CP // G
HW = H * W
ATT_N = np.sqrt(HW * HW * CG / CIN + HW * CG)


def setup_inputs():
    s = mx_kscale(CIN)
    r = np.sqrt(2.5 / ATT_N) / np.sqrt(CIN)
    return {"x": bf(np.random.standard_normal((B, CIN, H, W)) * s[None, :, None, None]),
            "Wt": bf(np.random.standard_normal((CP, CIN)) / np.sqrt(CIN) / s),
            "Wp": bf(np.random.standard_normal((CP, CIN)) * r / s),
            "Wg": bf(np.random.standard_normal((CP, CIN)) * r / s)}


def reference(x, Wt, Wp, Wg):
    xq = mxq(f64(x).reshape(B, CIN, HW), 1, "e4m3")
    t = mxq(f64(Wt), 1, "e4m3") @ xq
    p = mxq(f64(Wp), 1, "e4m3") @ xq
    g = mxq(f64(Wg), 1, "e4m3") @ xq
    t = t.reshape(B, G, CG * HW)
    p = p.reshape(B, G, CG * HW)
    g = g.reshape(B, G, CG * HW)
    att = (p * g).sum(-1, keepdims=True)
    return (att * t).reshape(B, G, CG, HW)

@@ -1,0 +1,224 @@
+from contextlib import ExitStack
+
+import concourse.mybir as mybir
+from concourse.masks import make_identity
+
+F32 = mybir.dt.float32
+BF16 = mybir.dt.bfloat16
+U32 = mybir.dt.uint32
+U8 = mybir.dt.uint8
+FP8X4 = mybir.dt.float8_e4m3fn_x4
+MULT = mybir.AluOpType.mult
+ADD = mybir.AluOpType.add
+COPY = mybir.ActivationFunctionType.Copy
+
+P = 128
+IMAGES = 3
+CIN = 2048
+HW = 256
+CP = 1024
+GROUPS = 2
+PASSES = CIN // 512
+UNITS = CP // P
+UPG = UNITS // GROUPS
+PG_PAIRS = UNITS
+T_PAIRS = UNITS // 2
+PAIRS = PG_PAIRS + T_PAIRS
+
+FLOPS = 2 * 3 * CP * CIN * IMAGES * HW
+
+
+def tile_spatialcgnl_pa_kernel(tc, x, Wt, Wp, Wg, out):
+    nc = tc.nc
+    with ExitStack() as ctx:
+        const = ctx.enter_context(tc.tile_pool(name="const", bufs=1))
+        xraw_pool = ctx.enter_context(tc.tile_pool(name="xraw", bufs=IMAGES))
+        xgrp_pool = ctx.enter_context(tc.tile_pool(name="xgrp", bufs=2))
+        wraw_pool = ctx.enter_context(tc.tile_pool(name="wraw", bufs=2 * PAIRS))
+        wgrp_pool = ctx.enter_context(tc.tile_pool(name="wgrp", bufs=4))
+        wq_pool = ctx.enter_context(tc.tile_pool(name="wq", bufs=10))
+        small = ctx.enter_context(tc.tile_pool(name="small", bufs=4))
+        tp_pool = ctx.enter_context(tc.psum_pool(name="tp", bufs=4))
+        acc_pool = ctx.enter_context(tc.psum_pool(name="acc", bufs=4))
+        ctx.enter_context(tc.manual_schedule())
+
+        def w_block(pair, s):
+            if pair < PG_PAIRS:
+                w, unit = (Wp, Wg)[s], pair
+            else:
+                w, unit = Wt, 2 * (pair - PG_PAIRS) + s
+            view = w.rearrange("(j p a) k -> j a p k", j=GROUPS, p=P, a=UPG)
+            return view[unit // UPG, unit % UPG]
+
+        xraw = [xraw_pool.tile([P, PASSES, 4, HW], BF16, name="xraw%d" % b, tag="xraw") for b in range(IMAGES)]
+        wraw = [
+            [wraw_pool.tile([P, CIN], BF16, name="wraw%d_%d" % (j, s), tag="wraw") for s in range(2)]
+            for j in range(PAIRS)
+        ]
+
+        def load_x(b):
+            src = x[b].rearrange("(c p e) h w -> p c (e h w)", c=2 * PASSES, p=P, e=2)
+            dst = xraw[b][:].rearrange("p g (u e) n -> p (g u) (e n)", u=2, e=2)
+            for h in range(2):
+                nc.sync.dma_start(out=dst[:, 4 * h : 4 * h + 4, :], in_=src[:, 4 * h : 4 * h + 4, :])
+
+        def load_w(j):
+            for s in range(2):
+                nc.sync.dma_start(out=wraw[j][s][:], in_=w_block(j, s))
+
+        load_x(0)
+        load_w(0)
+        load_w(1)
+        load_x(1)
+        load_x(2)
+        for j in range(2, PAIRS):
+            load_w(j)
+
+        ident = const.tile([P, P], F32)
+        make_identity(nc, ident[:])
+        ones = const.tile([P, P], F32)
+        nc.vector.memset(ones[:], 1.0)
+        part = const.tile([P, PG_PAIRS * IMAGES], F32)
+        att = const.tile([P, GROUPS * IMAGES], F32)
+        xc = [const.tile([P, PASSES * HW], U32, name="xc%d" % b, align_bytes=64) for b in range(IMAGES)]
+        xs = [const.tile([P, PASSES * HW], U8, name="xs%d" % b, align_bytes=64) for b in range(IMAGES)]
+
+        wc = {}
+        ws = {}
+        wgrp = {}
+        acc = {}
+
+        def prep_x(b):
+            xgrp = xgrp_pool.tile([P, PASSES, HW, 4], BF16, name="xgrp%d" % b, tag="xgrp", align_bytes=64)
+
+            def regroup(engine_copy, g):
+                engine_copy(
+                    out=xgrp[:, g].rearrange("p (c i) t -> p c t i", i=4),
+                    in_=xraw[b][:, g].rearrange("p t (c i) -> p c t i", i=4),
+                )
+
+            def quantise(h):
+                nc.vector.quantize_mx(
+                    out=xc[b][:, 512 * h : 512 * h + 512].bitcast(FP8X4),
+                    scales=xs[b][:, 512 * h : 512 * h + 512],
+                    in_=xgrp[:, 2 * h : 2 * h + 2].rearrange("p g n t -> p (g n t)"),
+                )
+
+            regroup(nc.vector.tensor_copy, 0)
+            regroup(nc.vector.tensor_copy, 1)
+            regroup(nc.scalar.copy, 3)
+            regroup(nc.vector.tensor_copy, 2)
+            quantise(0)
+            quantise(1)
+
+        def transposes(j):
+            for s in range(2):
+                words = wraw[j][s][:].bitcast(F32)
+                grp = wgrp_pool.tile([P, CIN], BF16, name="wgrp%d_%d" % (j, s), tag="wgrp", align_bytes=64)
+                wgrp[(j, s)] = grp
+                for h in range(2):
+                    tp = tp_pool.tile([P, 4, P], F32, name="tp%d_%d_%d" % (j, s, h), tag="tp")
+                    for c in range(4):
+                        col = P * (4 * h + c)
+                        nc.tensor.transpose(tp[:, c, :], words[:, col : col + P], ident[:])
+                    nc.scalar.copy(
+                        out=grp[:].bitcast(F32)[:, 512 * h : 512 * h + 512].rearrange(
+                            "p (g m u) -> p g m u", g=2, m=P, u=2
+                        ),
+                        in_=tp[:].rearrange("p (g u) m -> p g m u", g=2, u=2),
+                    )
+
+        def quantise_w(j):
+            for s in range(2):
+                wc[(j, s)] = wq_pool.tile([P, PASSES * P], U32, name="wc%d_%d" % (j, s), tag="wc", align_bytes=64)
+                ws[(j, s)] = wq_pool.tile([P, PASSES * P], U8, name="ws%d_%d" % (j, s), tag="ws", align_bytes=64)
+                nc.vector.quantize_mx(
+                    out=wc[(j, s)][:].bitcast(FP8X4), scales=ws[(j, s)][:], in_=wgrp[(j, s)][:]
+                )
+
+        def job(j, b):
+            bank = acc_pool.tile([P, 2, HW], F32, name="acc%d_%d" % (j, b), tag="acc")
+            acc[(j, b)] = bank
+            for s in range(2):
+                for g in range(PASSES):
+                    nc.tensor.matmul_mx(
+                        out=bank[:, s, :],
+                        lhsT=wc[(j, s)][:, P * g : P * g + P].bitcast(FP8X4),
+                        lhsT_scale=ws[(j, s)][:, P * g : P * g + P],
+                        rhs=xc[b][:, HW * g : HW * g + HW].bitcast(FP8X4),
+                        rhs_scale=xs[b][:, HW * g : HW * g + HW],
+                        start=(g == 0),
+                        stop=(g == PASSES - 1),
+                    )
+
+        def drain(j, b):
+            bank = acc[(j, b)]
+            if j < PG_PAIRS:
+                p_sb = small.tile([P, HW], F32, name="p_sb%d_%d" % (j, b), tag="p_sb")
+                nc.scalar.copy(out=p_sb[:], in_=bank[:, 0, :])
+                prod = small.tile([P, HW], F32, name="prod%d_%d" % (j, b), tag="prod")
+                col = j * IMAGES + b
+                nc.vector.scalar_tensor_tensor(
+                    out=prod[:],
+                    in0=bank[:, 1, :],
+                    scalar=1.0,
+                    in1=p_sb[:],
+                    op0=MULT,
+                    op1=MULT,
+                    accum_out=part[:, col : col + 1],
+                )
+            else:
+                unit = 2 * (j - PG_PAIRS)
+                grp, a0 = unit // UPG, unit % UPG
+                col = grp * IMAGES + b
+                y_sb = small.tile([P, 2, HW], F32, name="y_sb%d_%d" % (j, b), tag="y_sb")
+                if b == 1:
+                    nc.scalar.activation(out=y_sb[:], in_=bank[:], func=COPY, scale=att[:, col : col + 1])
+                else:
+                    nc.vector.tensor_scalar(
+                        out=y_sb[:], in0=bank[:], scalar1=att[:, col : col + 1], scalar2=None, op0=MULT
+                    )
+                dst = out[b, grp].rearrange("(p a) n -> p a n", a=UPG)
+                nc.sync.dma_start(out=dst[:, a0 : a0 + 2, :], in_=y_sb[:])
+
+        def attention():
+            att_ps = tp_pool.tile([P, 4, P], F32, name="att_ps", tag="tp")
+            n = PG_PAIRS * IMAGES
+            nc.tensor.matmul(att_ps[:, 0, 0:n], lhsT=ones[:], rhs=part[:], start=True, stop=True)
+            nc.vector.tensor_reduce(
+                out=att[:].rearrange("p (j b) -> p j b", j=GROUPS),
+                in_=att_ps[:, 0, 0:n].rearrange("p (j i b) -> p j b i", j=GROUPS, i=UPG, b=IMAGES),
+                axis=mybir.AxisListType.X,
+                op=ADD,
+            )
+
+        prep_x(0)
+        transposes(0)
+        quantise_w(0)
+        transposes(1)
+        quantise_w(1)
+        job(0, 0)
+        job(1, 0)
+        prep_x(1)
+        drain(0, 0)
+        drain(1, 0)
+        job(0, 1)
+        job(1, 1)
+        prep_x(2)
+        drain(0, 1)
+        drain(1, 1)
+        job(0, 2)
+        job(1, 2)
+        drain(0, 2)
+        drain(1, 2)
+        transposes(2)
+        quantise_w(2)
+        for j in range(2, PAIRS):
+            if j + 1 < PAIRS:
+                transposes(j + 1)
+                if j == PG_PAIRS:
+                    attention()
+                quantise_w(j + 1)
+            for b in range(IMAGES):
+                job(j, b)
+                drain(j, b)

@@ -66,13 +66,10 @@ def tile_spatialcgnl_pa_kernel(tc, x, Wt, Wp, Wg, out):
             for s in range(2):
                 nc.sync.dma_start(out=wraw[j][s][:], in_=w_block(j, s))
 
-        load_x(0)
-        load_w(0)
-        load_w(1)
-        load_x(1)
-        load_x(2)
-        for j in range(2, PAIRS):
+        for j in range(PAIRS):
             load_w(j)
+            if j < IMAGES:
+                load_x(j)
 
         ident = const.tile([P, P], F32)
         make_identity(nc, ident[:])
@@ -192,9 +189,9 @@ def tile_spatialcgnl_pa_kernel(tc, x, Wt, Wp, Wg, out):
                 op=ADD,
             )
 
-        prep_x(0)
         transposes(0)
         quantise_w(0)
+        prep_x(0)
         transposes(1)
         quantise_w(1)
         job(0, 0)
@@ -202,18 +199,23 @@ def tile_spatialcgnl_pa_kernel(tc, x, Wt, Wp, Wg, out):
         prep_x(1)
         drain(0, 0)
         drain(1, 0)
+        transposes(2)
+        quantise_w(2)
         job(0, 1)
         job(1, 1)
         prep_x(2)
         drain(0, 1)
         drain(1, 1)
-        job(0, 2)
-        job(1, 2)
-        drain(0, 2)
-        drain(1, 2)
-        transposes(2)
-        quantise_w(2)
-        for j in range(2, PAIRS):
+        job(2, 0)
+        job(2, 1)
+        drain(2, 0)
+        drain(2, 1)
+        transposes(3)
+        quantise_w(3)
+        for j in range(3):
+            job(j, 2)
+            drain(j, 2)
+        for j in range(3, PAIRS):
             if j + 1 < PAIRS:
                 transposes(j + 1)
                 if j == PG_PAIRS:

@@ -108,7 +108,7 @@ def tile_spatialcgnl_pa_kernel(tc, x, Wt, Wp, Wg, out):
             quantise(0)
             quantise(1)
 
-        def transposes(j):
+        def transposes(j, share=False):
             for s in range(2):
                 words = wraw[j][s][:].bitcast(F32)
                 grp = wgrp_pool.tile([P, CIN], BF16, name="wgrp%d_%d" % (j, s), tag="wgrp", align_bytes=64)
@@ -118,7 +118,8 @@ def tile_spatialcgnl_pa_kernel(tc, x, Wt, Wp, Wg, out):
                     for c in range(4):
                         col = P * (4 * h + c)
                         nc.tensor.transpose(tp[:, c, :], words[:, col : col + P], ident[:])
-                    nc.scalar.copy(
+                    copy_out = nc.vector.tensor_copy if (share and h == 1) else nc.scalar.copy
+                    copy_out(
                         out=grp[:].bitcast(F32)[:, 512 * h : 512 * h + 512].rearrange(
                             "p (g m u) -> p g m u", g=2, m=P, u=2
                         ),
@@ -215,12 +216,19 @@ def tile_spatialcgnl_pa_kernel(tc, x, Wt, Wp, Wg, out):
         for j in range(3):
             job(j, 2)
             drain(j, 2)
-        for j in range(3, PAIRS):
-            if j + 1 < PAIRS:
-                transposes(j + 1)
-                if j == PG_PAIRS:
-                    attention()
-                quantise_w(j + 1)
+        for a in range(4, PAIRS, 2):
+            transposes(a, share=True)
+            transposes(a + 1, share=True)
+            quantise_w(a)
             for b in range(IMAGES):
-                job(j, b)
-                drain(j, b)
+                job(a - 1, b)
+                drain(a - 1, b)
+            quantise_w(a + 1)
+            for b in range(IMAGES):
+                job(a, b)
+                if a == PG_PAIRS and b == 0:
+                    attention()
+                drain(a, b)
+        for b in range(IMAGES):
+            job(PAIRS - 1, b)
+            drain(PAIRS - 1, b)

@@ -13,17 +13,20 @@ ADD = mybir.AluOpType.add
 COPY = mybir.ActivationFunctionType.Copy
 
 P = 128
+PACK = 4
+BANK = 512
 IMAGES = 3
 CIN = 2048
 HW = 256
 CP = 1024
 GROUPS = 2
-PASSES = CIN // 512
-UNITS = CP // P
-UPG = UNITS // GROUPS
-PG_PAIRS = UNITS
-T_PAIRS = UNITS // 2
+PASSES = CIN // (P * PACK)
+PANELS = CP // P
+PPG = PANELS // GROUPS
+PG_PAIRS = PANELS
+T_PAIRS = PANELS // 2
 PAIRS = PG_PAIRS + T_PAIRS
+START_PAIRS = IMAGES
 
 FLOPS = 2 * 3 * CP * CIN * IMAGES * HW
 
@@ -42,33 +45,34 @@ def tile_spatialcgnl_pa_kernel(tc, x, Wt, Wp, Wg, out):
         acc_pool = ctx.enter_context(tc.psum_pool(name="acc", bufs=4))
         ctx.enter_context(tc.manual_schedule())
 
-        def w_block(pair, s):
-            if pair < PG_PAIRS:
-                w, unit = (Wp, Wg)[s], pair
+        def panel_in_dram(j, s):
+            if j < PG_PAIRS:
+                w, panel = (Wp, Wg)[s], j
             else:
-                w, unit = Wt, 2 * (pair - PG_PAIRS) + s
-            view = w.rearrange("(j p a) k -> j a p k", j=GROUPS, p=P, a=UPG)
-            return view[unit // UPG, unit % UPG]
+                w, panel = Wt, 2 * (j - PG_PAIRS) + s
+            view = w.rearrange("(c p a) k -> c a p k", c=GROUPS, p=P, a=PPG)
+            return view[panel // PPG, panel % PPG]
 
-        xraw = [xraw_pool.tile([P, PASSES, 4, HW], BF16, name="xraw%d" % b, tag="xraw") for b in range(IMAGES)]
+        xraw = [xraw_pool.tile([P, PASSES, PACK, HW], BF16, name="xraw%d" % b, tag="xraw") for b in range(IMAGES)]
         wraw = [
             [wraw_pool.tile([P, CIN], BF16, name="wraw%d_%d" % (j, s), tag="wraw") for s in range(2)]
             for j in range(PAIRS)
         ]
 
         def load_x(b):
-            src = x[b].rearrange("(c p e) h w -> p c (e h w)", c=2 * PASSES, p=P, e=2)
+            src = x[b].rearrange("(g u p e) h w -> p (g u) (e h w)", g=PASSES, u=2, p=P, e=2)
             dst = xraw[b][:].rearrange("p g (u e) n -> p (g u) (e n)", u=2, e=2)
-            for h in range(2):
-                nc.sync.dma_start(out=dst[:, 4 * h : 4 * h + 4, :], in_=src[:, 4 * h : 4 * h + 4, :])
+            for half in range(2):
+                chunks = slice(PASSES * half, PASSES * half + PASSES)
+                nc.sync.dma_start(out=dst[:, chunks, :], in_=src[:, chunks, :])
 
         def load_w(j):
             for s in range(2):
-                nc.sync.dma_start(out=wraw[j][s][:], in_=w_block(j, s))
+                nc.sync.dma_start(out=wraw[j][s][:], in_=panel_in_dram(j, s))
 
         for j in range(PAIRS):
             load_w(j)
-            if j < IMAGES:
+            if j < START_PAIRS:
                 load_x(j)
 
         ident = const.tile([P, P], F32)
@@ -86,19 +90,20 @@ def tile_spatialcgnl_pa_kernel(tc, x, Wt, Wp, Wg, out):
         acc = {}
 
         def prep_x(b):
-            xgrp = xgrp_pool.tile([P, PASSES, HW, 4], BF16, name="xgrp%d" % b, tag="xgrp", align_bytes=64)
+            xgrp = xgrp_pool.tile([P, PASSES, HW, PACK], BF16, name="xgrp%d" % b, tag="xgrp", align_bytes=64)
 
             def regroup(engine_copy, g):
                 engine_copy(
-                    out=xgrp[:, g].rearrange("p (c i) t -> p c t i", i=4),
-                    in_=xraw[b][:, g].rearrange("p t (c i) -> p c t i", i=4),
+                    out=xgrp[:, g].rearrange("p (v f) t -> p v t f", f=4),
+                    in_=xraw[b][:, g].rearrange("p t (v f) -> p v t f", f=4),
                 )
 
-            def quantise(h):
+            def quantise(half):
+                cols = slice(2 * HW * half, 2 * HW * half + 2 * HW)
                 nc.vector.quantize_mx(
-                    out=xc[b][:, 512 * h : 512 * h + 512].bitcast(FP8X4),
-                    scales=xs[b][:, 512 * h : 512 * h + 512],
-                    in_=xgrp[:, 2 * h : 2 * h + 2].rearrange("p g n t -> p (g n t)"),
+                    out=xc[b][:, cols].bitcast(FP8X4),
+                    scales=xs[b][:, cols],
+                    in_=xgrp[:, 2 * half : 2 * half + 2].rearrange("p g n t -> p (g n t)"),
                 )
 
             regroup(nc.vector.tensor_copy, 0)
@@ -108,19 +113,18 @@ def tile_spatialcgnl_pa_kernel(tc, x, Wt, Wp, Wg, out):
             quantise(0)
             quantise(1)
 
-        def transposes(j, share=False):
+        def transposes(j):
             for s in range(2):
                 words = wraw[j][s][:].bitcast(F32)
-                grp = wgrp_pool.tile([P, CIN], BF16, name="wgrp%d_%d" % (j, s), tag="wgrp", align_bytes=64)
-                wgrp[(j, s)] = grp
-                for h in range(2):
-                    tp = tp_pool.tile([P, 4, P], F32, name="tp%d_%d_%d" % (j, s, h), tag="tp")
-                    for c in range(4):
-                        col = P * (4 * h + c)
-                        nc.tensor.transpose(tp[:, c, :], words[:, col : col + P], ident[:])
-                    copy_out = nc.vector.tensor_copy if (share and h == 1) else nc.scalar.copy
-                    copy_out(
-                        out=grp[:].bitcast(F32)[:, 512 * h : 512 * h + 512].rearrange(
+                regrouped = wgrp_pool.tile([P, CIN], BF16, name="wgrp%d_%d" % (j, s), tag="wgrp", align_bytes=64)
+                wgrp[(j, s)] = regrouped
+                for half in range(2):
+                    tp = tp_pool.tile([P, 4, P], F32, name="tp%d_%d_%d" % (j, s, half), tag="tp")
+                    for slot in range(4):
+                        first = BANK * half + P * slot
+                        nc.tensor.transpose(tp[:, slot, :], words[:, first : first + P], ident[:])
+                    nc.scalar.copy(
+                        out=regrouped[:].bitcast(F32)[:, BANK * half : BANK * half + BANK].rearrange(
                             "p (g m u) -> p g m u", g=2, m=P, u=2
                         ),
                         in_=tp[:].rearrange("p (g u) m -> p g m u", g=2, u=2),
@@ -155,7 +159,6 @@ def tile_spatialcgnl_pa_kernel(tc, x, Wt, Wp, Wg, out):
                 p_sb = small.tile([P, HW], F32, name="p_sb%d_%d" % (j, b), tag="p_sb")
                 nc.scalar.copy(out=p_sb[:], in_=bank[:, 0, :])
                 prod = small.tile([P, HW], F32, name="prod%d_%d" % (j, b), tag="prod")
-                col = j * IMAGES + b
                 nc.vector.scalar_tensor_tensor(
                     out=prod[:],
                     in0=bank[:, 1, :],
@@ -163,72 +166,53 @@ def tile_spatialcgnl_pa_kernel(tc, x, Wt, Wp, Wg, out):
                     in1=p_sb[:],
                     op0=MULT,
                     op1=MULT,
-                    accum_out=part[:, col : col + 1],
+                    accum_out=part[:, j * IMAGES + b : j * IMAGES + b + 1],
                 )
             else:
-                unit = 2 * (j - PG_PAIRS)
-                grp, a0 = unit // UPG, unit % UPG
-                col = grp * IMAGES + b
+                panel = 2 * (j - PG_PAIRS)
+                c, a = panel // PPG, panel % PPG
+                factor = att[:, c * IMAGES + b : c * IMAGES + b + 1]
                 y_sb = small.tile([P, 2, HW], F32, name="y_sb%d_%d" % (j, b), tag="y_sb")
                 if b == 1:
-                    nc.scalar.activation(out=y_sb[:], in_=bank[:], func=COPY, scale=att[:, col : col + 1])
+                    nc.scalar.activation(out=y_sb[:], in_=bank[:], func=COPY, scale=factor)
                 else:
-                    nc.vector.tensor_scalar(
-                        out=y_sb[:], in0=bank[:], scalar1=att[:, col : col + 1], scalar2=None, op0=MULT
-                    )
-                dst = out[b, grp].rearrange("(p a) n -> p a n", a=UPG)
-                nc.sync.dma_start(out=dst[:, a0 : a0 + 2, :], in_=y_sb[:])
+                    nc.vector.tensor_scalar(out=y_sb[:], in0=bank[:], scalar1=factor, scalar2=None, op0=MULT)
+                dst = out[b, c].rearrange("(p a) n -> p a n", a=PPG)
+                nc.sync.dma_start(out=dst[:, a : a + 2, :], in_=y_sb[:])
 
         def attention():
             att_ps = tp_pool.tile([P, 4, P], F32, name="att_ps", tag="tp")
-            n = PG_PAIRS * IMAGES
-            nc.tensor.matmul(att_ps[:, 0, 0:n], lhsT=ones[:], rhs=part[:], start=True, stop=True)
+            sums = att_ps[:, 0, 0 : PG_PAIRS * IMAGES]
+            nc.tensor.matmul(sums, lhsT=ones[:], rhs=part[:], start=True, stop=True)
             nc.vector.tensor_reduce(
-                out=att[:].rearrange("p (j b) -> p j b", j=GROUPS),
-                in_=att_ps[:, 0, 0:n].rearrange("p (j i b) -> p j b i", j=GROUPS, i=UPG, b=IMAGES),
+                out=att[:].rearrange("p (c b) -> p c b", c=GROUPS),
+                in_=sums.rearrange("p (c a b) -> p c b a", c=GROUPS, a=PPG, b=IMAGES),
                 axis=mybir.AxisListType.X,
                 op=ADD,
             )
 
+        def run(jobs, between=None):
+            for j, b in jobs:
+                job(j, b)
+            if between is not None:
+                prep_x(between)
+            for j, b in jobs:
+                drain(j, b)
+
         transposes(0)
         quantise_w(0)
         prep_x(0)
-        transposes(1)
-        quantise_w(1)
-        job(0, 0)
-        job(1, 0)
-        prep_x(1)
-        drain(0, 0)
-        drain(1, 0)
-        transposes(2)
-        quantise_w(2)
-        job(0, 1)
-        job(1, 1)
-        prep_x(2)
-        drain(0, 1)
-        drain(1, 1)
-        job(2, 0)
-        job(2, 1)
-        drain(2, 0)
-        drain(2, 1)
-        transposes(3)
-        quantise_w(3)
-        for j in range(3):
-            job(j, 2)
-            drain(j, 2)
-        for a in range(4, PAIRS, 2):
-            transposes(a, share=True)
-            transposes(a + 1, share=True)
-            quantise_w(a)
-            for b in range(IMAGES):
-                job(a - 1, b)
-                drain(a - 1, b)
-            quantise_w(a + 1)
-            for b in range(IMAGES):
-                job(a, b)
-                if a == PG_PAIRS and b == 0:
+        for r in range(1, START_PAIRS + 1):
+            transposes(r)
+            quantise_w(r)
+            run([(j, r - 1) for j in range(r)], between=(r if r < IMAGES else None))
+            if r < START_PAIRS:
+                run([(r, b) for b in range(r)])
+        for j in range(START_PAIRS, PAIRS):
+            if j + 1 < PAIRS:
+                transposes(j + 1)
+                if j == PG_PAIRS:
                     attention()
-                drain(a, b)
-        for b in range(IMAGES):
-            job(PAIRS - 1, b)
-            drain(PAIRS - 1, b)
+                quantise_w(j + 1)
+            for b in range(IMAGES):
+                run([(j, b)])

from contextlib import ExitStack

import concourse.mybir as mybir
from concourse.masks import make_identity

F32 = mybir.dt.float32
BF16 = mybir.dt.bfloat16
U32 = mybir.dt.uint32
U8 = mybir.dt.uint8
FP8X4 = mybir.dt.float8_e4m3fn_x4
MULT = mybir.AluOpType.mult
ADD = mybir.AluOpType.add
COPY = mybir.ActivationFunctionType.Copy

P = 128
PACK = 4
BANK = 512
IMAGES = 3
CIN = 2048
HW = 256
CP = 1024
GROUPS = 2
PASSES = CIN // (P * PACK)
PANELS = CP // P
PPG = PANELS // GROUPS
PG_PAIRS = PANELS
T_PAIRS = PANELS // 2
PAIRS = PG_PAIRS + T_PAIRS
START_PAIRS = IMAGES

FLOPS = 2 * 3 * CP * CIN * IMAGES * HW


def tile_spatialcgnl_pa_kernel(tc, x, Wt, Wp, Wg, out):
    nc = tc.nc
    with ExitStack() as ctx:
        const = ctx.enter_context(tc.tile_pool(name="const", bufs=1))
        xraw_pool = ctx.enter_context(tc.tile_pool(name="xraw", bufs=IMAGES))
        xgrp_pool = ctx.enter_context(tc.tile_pool(name="xgrp", bufs=2))
        wraw_pool = ctx.enter_context(tc.tile_pool(name="wraw", bufs=2 * PAIRS))
        wgrp_pool = ctx.enter_context(tc.tile_pool(name="wgrp", bufs=4))
        wq_pool = ctx.enter_context(tc.tile_pool(name="wq", bufs=10))
        small = ctx.enter_context(tc.tile_pool(name="small", bufs=4))
        tp_pool = ctx.enter_context(tc.psum_pool(name="tp", bufs=4))
        acc_pool = ctx.enter_context(tc.psum_pool(name="acc", bufs=4))
        ctx.enter_context(tc.manual_schedule())

        def panel_in_dram(j, s):
            if j < PG_PAIRS:
                w, panel = (Wp, Wg)[s], j
            else:
                w, panel = Wt, 2 * (j - PG_PAIRS) + s
            view = w.rearrange("(c p a) k -> c a p k", c=GROUPS, p=P, a=PPG)
            return view[panel // PPG, panel % PPG]

        xraw = [xraw_pool.tile([P, PASSES, PACK, HW], BF16, name="xraw%d" % b, tag="xraw") for b in range(IMAGES)]
        wraw = [
            [wraw_pool.tile([P, CIN], BF16, name="wraw%d_%d" % (j, s), tag="wraw") for s in range(2)]
            for j in range(PAIRS)
        ]

        def load_x(b):
            src = x[b].rearrange("(g u p e) h w -> p (g u) (e h w)", g=PASSES, u=2, p=P, e=2)
            dst = xraw[b][:].rearrange("p g (u e) n -> p (g u) (e n)", u=2, e=2)
            for half in range(2):
                chunks = slice(PASSES * half, PASSES * half + PASSES)
                nc.sync.dma_start(out=dst[:, chunks, :], in_=src[:, chunks, :])

        def load_w(j):
            for s in range(2):
                nc.sync.dma_start(out=wraw[j][s][:], in_=panel_in_dram(j, s))

        for j in range(PAIRS):
            load_w(j)
            if j < START_PAIRS:
                load_x(j)

        ident = const.tile([P, P], F32)
        make_identity(nc, ident[:])
        ones = const.tile([P, P], F32)
        nc.vector.memset(ones[:], 1.0)
        part = const.tile([P, PG_PAIRS * IMAGES], F32)
        att = const.tile([P, GROUPS * IMAGES], F32)
        xc = [const.tile([P, PASSES * HW], U32, name="xc%d" % b, align_bytes=64) for b in range(IMAGES)]
        xs = [const.tile([P, PASSES * HW], U8, name="xs%d" % b, align_bytes=64) for b in range(IMAGES)]

        wc = {}
        ws = {}
        wgrp = {}
        acc = {}

        def prep_x(b):
            xgrp = xgrp_pool.tile([P, PASSES, HW, PACK], BF16, name="xgrp%d" % b, tag="xgrp", align_bytes=64)

            def regroup(engine_copy, g):
                engine_copy(
                    out=xgrp[:, g].rearrange("p (v f) t -> p v t f", f=4),
                    in_=xraw[b][:, g].rearrange("p t (v f) -> p v t f", f=4),
                )

            def quantise(half):
                cols = slice(2 * HW * half, 2 * HW * half + 2 * HW)
                nc.vector.quantize_mx(
                    out=xc[b][:, cols].bitcast(FP8X4),
                    scales=xs[b][:, cols],
                    in_=xgrp[:, 2 * half : 2 * half + 2].rearrange("p g n t -> p (g n t)"),
                )

            regroup(nc.vector.tensor_copy, 0)
            regroup(nc.vector.tensor_copy, 1)
            regroup(nc.scalar.copy, 3)
            regroup(nc.vector.tensor_copy, 2)
            quantise(0)
            quantise(1)

        def transposes(j):
            for s in range(2):
                words = wraw[j][s][:].bitcast(F32)
                regrouped = wgrp_pool.tile([P, CIN], BF16, name="wgrp%d_%d" % (j, s), tag="wgrp", align_bytes=64)
                wgrp[(j, s)] = regrouped
                for half in range(2):
                    tp = tp_pool.tile([P, 4, P], F32, name="tp%d_%d_%d" % (j, s, half), tag="tp")
                    for slot in range(4):
                        first = BANK * half + P * slot
                        nc.tensor.transpose(tp[:, slot, :], words[:, first : first + P], ident[:])
                    nc.scalar.copy(
                        out=regrouped[:].bitcast(F32)[:, BANK * half : BANK * half + BANK].rearrange(
                            "p (g m u) -> p g m u", g=2, m=P, u=2
                        ),
                        in_=tp[:].rearrange("p (g u) m -> p g m u", g=2, u=2),
                    )

        def quantise_w(j):
            for s in range(2):
                wc[(j, s)] = wq_pool.tile([P, PASSES * P], U32, name="wc%d_%d" % (j, s), tag="wc", align_bytes=64)
                ws[(j, s)] = wq_pool.tile([P, PASSES * P], U8, name="ws%d_%d" % (j, s), tag="ws", align_bytes=64)
                nc.vector.quantize_mx(
                    out=wc[(j, s)][:].bitcast(FP8X4), scales=ws[(j, s)][:], in_=wgrp[(j, s)][:]
                )

        def job(j, b):
            bank = acc_pool.tile([P, 2, HW], F32, name="acc%d_%d" % (j, b), tag="acc")
            acc[(j, b)] = bank
            for s in range(2):
                for g in range(PASSES):
                    nc.tensor.matmul_mx(
                        out=bank[:, s, :],
                        lhsT=wc[(j, s)][:, P * g : P * g + P].bitcast(FP8X4),
                        lhsT_scale=ws[(j, s)][:, P * g : P * g + P],
                        rhs=xc[b][:, HW * g : HW * g + HW].bitcast(FP8X4),
                        rhs_scale=xs[b][:, HW * g : HW * g + HW],
                        start=(g == 0),
                        stop=(g == PASSES - 1),
                    )

        def drain(j, b):
            bank = acc[(j, b)]
            if j < PG_PAIRS:
                p_sb = small.tile([P, HW], F32, name="p_sb%d_%d" % (j, b), tag="p_sb")
                nc.scalar.copy(out=p_sb[:], in_=bank[:, 0, :])
                prod = small.tile([P, HW], F32, name="prod%d_%d" % (j, b), tag="prod")
                nc.vector.scalar_tensor_tensor(
                    out=prod[:],
                    in0=bank[:, 1, :],
                    scalar=1.0,
                    in1=p_sb[:],
                    op0=MULT,
                    op1=MULT,
                    accum_out=part[:, j * IMAGES + b : j * IMAGES + b + 1],
                )
            else:
                panel = 2 * (j - PG_PAIRS)
                c, a = panel // PPG, panel % PPG
                factor = att[:, c * IMAGES + b : c * IMAGES + b + 1]
                y_sb = small.tile([P, 2, HW], F32, name="y_sb%d_%d" % (j, b), tag="y_sb")
                if b == 1:
                    nc.scalar.activation(out=y_sb[:], in_=bank[:], func=COPY, scale=factor)
                else:
                    nc.vector.tensor_scalar(out=y_sb[:], in0=bank[:], scalar1=factor, scalar2=None, op0=MULT)
                dst = out[b, c].rearrange("(p a) n -> p a n", a=PPG)
                nc.sync.dma_start(out=dst[:, a : a + 2, :], in_=y_sb[:])

        def attention():
            att_ps = tp_pool.tile([P, 4, P], F32, name="att_ps", tag="tp")
            sums = att_ps[:, 0, 0 : PG_PAIRS * IMAGES]
            nc.tensor.matmul(sums, lhsT=ones[:], rhs=part[:], start=True, stop=True)
            nc.vector.tensor_reduce(
                out=att[:].rearrange("p (c b) -> p c b", c=GROUPS),
                in_=sums.rearrange("p (c a b) -> p c b a", c=GROUPS, a=PPG, b=IMAGES),
                axis=mybir.AxisListType.X,
                op=ADD,
            )

        def run(jobs, between=None):
            for j, b in jobs:
                job(j, b)
            if between is not None:
                prep_x(between)
            for j, b in jobs:
                drain(j, b)

        transposes(0)
        quantise_w(0)
        prep_x(0)
        for r in range(1, START_PAIRS + 1):
            transposes(r)
            quantise_w(r)
            run([(j, r - 1) for j in range(r)], between=(r if r < IMAGES else None))
            if r < START_PAIRS:
                run([(r, b) for b in range(r)])
        for j in range(START_PAIRS, PAIRS):
            if j + 1 < PAIRS:
                transposes(j + 1)
                if j == PG_PAIRS:
                    attention()
                quantise_w(j + 1)
            for b in range(IMAGES):
                run([(j, b)])
